import numpy as np
import ml_dtypes


BF16 = ml_dtypes.bfloat16


def bf(x):
    return np.asarray(x, np.float32).astype(BF16)


def f64(x):
    return np.asarray(x).astype(np.float64)


E2M1 = np.array([0.0, 0.5, 1.0, 1.5, 2.0, 3.0, 4.0, 6.0, -0.0, -0.5, -1.0, -1.5, -2.0, -3.0, -4.0, -6.0])


def pack_weight(w, fmt):
    k, n = w.shape
    w = f64(bf(w)).reshape(k // 32, 32, n)
    amax = np.abs(w).max(1)
    if fmt == "e4m3":
        byte = np.frexp(amax)[1] - 1 + 127 - 7
    else:
        mant, ex = np.frexp(amax / 6.0)
        byte = np.where(mant > 0.5, ex, ex - 1) + 127
    byte = np.clip(np.where(amax > 0, byte, 1), 1, 254)
    scaled = (w * np.exp2(127.0 - byte)[:, None, :]).reshape(k, n).astype(np.float32)
    by_word = np.ascontiguousarray(scaled.reshape(k // 512, 128, 4, n).transpose(0, 1, 3, 2))
    if fmt == "e4m3":
        words = by_word.astype(ml_dtypes.float8_e4m3fn).view(np.uint8)
    else:
        c = by_word.astype(ml_dtypes.float4_e2m1fn).view(np.uint8) & 0xF
        words = c[..., 0::2] | (c[..., 1::2] << 4)
    return np.ascontiguousarray(words), np.ascontiguousarray(byte.astype(np.uint8).reshape(k // 512, 16, n))


def unpack_weight(words, scales, fmt):
    g, p, n, _ = words.shape
    if fmt == "e4m3":
        vals = np.ascontiguousarray(words).view(ml_dtypes.float8_e4m3fn).astype(np.float64)
    else:
        nib = np.empty((g, p, n, 4), np.uint8)
        nib[..., 0::2] = words & 0xF
        nib[..., 1::2] = words >> 4
        vals = E2M1[nib]
    vals = vals * np.repeat(np.exp2(scales.astype(np.float64) - 127.0), 8, axis=1)[..., None]
    return vals.transpose(0, 1, 3, 2).reshape(g * 512, n)

def pack4(w):
    words, scales = pack_weight(w, "e2m1")
    return words.reshape(words.shape[0], 128, -1), scales


def unpack4(words, scales):
    return unpack_weight(words.reshape(words.shape[0], 128, -1, 2), scales, "e2m1")


def kspread(k):
    return np.exp2(np.repeat(np.random.randint(-6, 7, k // 32), 32).astype(np.float64))


B, S, D, H, DH, F = 1, 512, 3072, 8, 128, 12288
INNER = H * DH
HALF = DH // 2
EPS = 1e-5


def rmsnorm(u, g):
    var = np.mean(np.square(u), axis=-1, keepdims=True)
    return u * (1.0 / np.sqrt(var + EPS)) * g


def rope_interleaved(u, cos, sin):
    u1 = u[..., 0::2]
    u2 = u[..., 1::2]
    c = cos[None, :, None, :]
    s = sin[None, :, None, :]
    o1 = u1 * c - u2 * s
    o2 = u2 * c + u1 * s
    return np.stack([o1, o2], axis=-1).reshape(u.shape)


def setup_inputs():
    s = kspread(D)
    ang = np.random.uniform(0.0, 2.0 * np.pi, (S, HALF))
    hidden_states = np.random.standard_normal((B, S, D)) * s
    hidden_states_words, hidden_states_scales = pack4(hidden_states.reshape(B * S, D).T)
    w_q_words, w_q_scales = pack4(np.random.standard_normal((D, INNER)) * 0.02 / np.sqrt(D) / s[:, None])
    w_k_words, w_k_scales = pack4(np.random.standard_normal((D, INNER)) * 0.02 / np.sqrt(D) / s[:, None])
    w_v_words, w_v_scales = pack4(np.random.standard_normal((D, INNER)) * 3.0 / np.sqrt(D) / s[:, None])
    return {"hidden_states_words": hidden_states_words,
            "hidden_states_scales": hidden_states_scales,
            "w_q_words": w_q_words,
            "w_q_scales": w_q_scales,
            "w_k_words": w_k_words,
            "w_k_scales": w_k_scales,
            "w_v_words": w_v_words,
            "w_v_scales": w_v_scales,
            "norm_q_w": bf(1.0 + 0.1 * np.random.standard_normal(DH)),
            "norm_k_w": bf(1.0 + 0.1 * np.random.standard_normal(DH)),
            "cos": bf(np.cos(ang)),
            "sin": bf(np.sin(ang))}


def reference(hidden_states_words, hidden_states_scales, w_q_words, w_q_scales, w_k_words, w_k_scales, w_v_words, w_v_scales, norm_q_w, norm_k_w, cos, sin):
    xq = unpack4(hidden_states_words, hidden_states_scales).T.reshape(B, S, D)
    q = (xq @ unpack4(w_q_words, w_q_scales)).reshape(B, S, H, DH)
    k = (xq @ unpack4(w_k_words, w_k_scales)).reshape(B, S, H, DH)
    v = (xq @ unpack4(w_v_words, w_v_scales)).reshape(B, S, H, DH)
    q = rmsnorm(q, f64(norm_q_w))
    k = rmsnorm(k, f64(norm_k_w))
    q = rope_interleaved(q, f64(cos), f64(sin))
    k = rope_interleaved(k, f64(cos), f64(sin))
    return q, k, v

@@ -1,0 +1,264 @@
+from contextlib import ExitStack
+
+import concourse.mybir as mybir
+
+F32 = mybir.dt.float32
+BF16 = mybir.dt.bfloat16
+U8 = mybir.dt.uint8
+I32 = mybir.dt.int32
+FP4X4 = mybir.dt.float4_e2m1fn_x4
+ACT = mybir.ActivationFunctionType
+ALU = mybir.AluOpType
+
+P = 128
+TOKENS, D_IN, HEADS, DH = 512, 3072, 8, 128
+INNER = HEADS * DH
+PASSES = D_IN // 512
+TOKEN_TILES = TOKENS // P
+BLOCK = 512
+BLOCK_HEADS = BLOCK // DH
+PAIRS = DH // 2
+EPS = 1e-5
+FLOPS = 2 * TOKENS * D_IN * 3 * INNER
+
+HEAD_PASSES = 3
+WARM_UPS = 7
+
+
+def tile_flux2parallelselfattention_pa_kernel(
+    tc,
+    hidden_words,
+    hidden_scales,
+    w_q_words,
+    w_q_scales,
+    w_k_words,
+    w_k_scales,
+    w_v_words,
+    w_v_scales,
+    norm_q_w,
+    norm_k_w,
+    cos,
+    sin,
+    out_q,
+    out_k,
+    out_v,
+):
+    nc = tc.nc
+    outs = {
+        "q": out_q.rearrange("b s h d -> (b s) (h d)"),
+        "k": out_k.rearrange("b s h d -> (b s) (h d)"),
+        "v": out_v.rearrange("b s h d -> (b s) (h d)"),
+    }
+
+    with ExitStack() as ctx:
+        keep = ctx.enter_context(tc.tile_pool(name="keep", bufs=1))
+        work = ctx.enter_context(tc.tile_pool(name="work", bufs=3))
+        res = ctx.enter_context(tc.tile_pool(name="res", bufs=6))
+        psum = ctx.enter_context(tc.psum_pool(name="psum", bufs=8))
+        ctx.enter_context(tc.manual_schedule())
+
+        x_codes = keep.tile([P, PASSES, 2 * TOKENS], U8, align_bytes=64)
+        x_planes = keep.tile([P, PASSES, TOKENS], U8, align_bytes=64)
+        q0_codes = keep.tile([P, PASSES, 2 * BLOCK], U8, align_bytes=64)
+        q0_planes = keep.tile([P, PASSES, BLOCK], U8, align_bytes=64)
+        q1_codes = keep.tile([P, PASSES, 2 * BLOCK], U8, align_bytes=64)
+        q1_planes = keep.tile([P, PASSES, BLOCK], U8, align_bytes=64)
+        k_codes = keep.tile([P, PASSES, 2 * INNER], U8, align_bytes=64)
+        k_planes = keep.tile([P, PASSES, INNER], U8, align_bytes=64)
+        v_codes = keep.tile([P, PASSES, 2 * INNER], U8, align_bytes=64)
+        v_planes = keep.tile([P, PASSES, INNER], U8, align_bytes=64)
+        warm = keep.tile([P, BLOCK], BF16)
+        gain_rows = keep.tile([P, 2 * DH], BF16)
+        cos_raw = keep.tile([P, TOKEN_TILES, PAIRS], BF16)
+        sin_raw = keep.tile([P, TOKEN_TILES, PAIRS], BF16)
+        gains = keep.tile([P, 2, DH], F32)
+        cos_pairs = keep.tile([P, TOKEN_TILES, DH], F32)
+        sin_pairs = keep.tile([P, TOKEN_TILES, DH], F32)
+        q_cos = keep.tile([P, TOKEN_TILES, DH], F32)
+        q_sin = keep.tile([P, TOKEN_TILES, DH], F32)
+        k_cos = keep.tile([P, TOKEN_TILES, DH], F32)
+        k_sin = keep.tile([P, TOKEN_TILES, DH], F32)
+        table_seed = keep.tile([P, 1], F32)
+
+        def zero(engine, planes, g0, g1):
+            engine.memset(planes[:, g0:g1, :].bitcast(I32), 0)
+
+        def load_codes(tile, words, g0, g1, c0, c1):
+            nc.sync.dma_start(
+                out=tile[:, g0:g1, :],
+                in_=words[g0:g1, :, 2 * c0 : 2 * c1].rearrange("g p n -> p g n"),
+            )
+
+        def load_scales(planes, scales, g0, g1, c0, c1):
+            for quad in range(4):
+                nc.sync.dma_start(
+                    out=planes[32 * quad : 32 * quad + 4, g0:g1, :].bitcast(I32),
+                    in_=scales[g0:g1, 4 * quad : 4 * quad + 4, c0:c1].rearrange("g r n -> r g n").bitcast(I32),
+                )
+
+        head = HEAD_PASSES
+        zero(nc.vector, x_planes, 0, head)
+        zero(nc.gpsimd, q0_planes, 0, head)
+        nc.vector.memset(warm[:], 1.0)
+        nc.gpsimd.memset(gain_rows[:], 0.0)
+        nc.vector.memset(table_seed[:], 1.0)
+        zero(nc.vector, x_planes, head, PASSES)
+        zero(nc.vector, q0_planes, head, PASSES)
+        zero(nc.vector, q1_planes, 0, PASSES)
+
+        nc.gpsimd.dma_start(out=gain_rows[0:1, 0:DH], in_=norm_q_w.unsqueeze(0))
+        nc.gpsimd.dma_start(out=gain_rows[0:1, DH : 2 * DH], in_=norm_k_w.unsqueeze(0))
+        nc.gpsimd.dma_start(out=cos_raw[:], in_=cos.rearrange("(t p) i -> p t i", p=P))
+        nc.gpsimd.dma_start(out=sin_raw[:], in_=sin.rearrange("(t p) i -> p t i", p=P))
+        zero(nc.gpsimd, v_planes, 0, PASSES)
+        zero(nc.gpsimd, k_planes, 0, PASSES)
+
+        load_codes(x_codes, hidden_words, 0, 1, 0, TOKENS)
+        load_codes(q0_codes, w_q_words, 0, 1, 0, BLOCK)
+        load_scales(x_planes, hidden_scales, 0, head, 0, TOKENS)
+        load_scales(q0_planes, w_q_scales, 0, head, 0, BLOCK)
+        load_codes(x_codes, hidden_words, 1, head, 0, TOKENS)
+        load_codes(q0_codes, w_q_words, 1, head, 0, BLOCK)
+        load_scales(x_planes, hidden_scales, head, PASSES, 0, TOKENS)
+        load_codes(x_codes, hidden_words, head, PASSES, 0, TOKENS)
+        load_codes(q0_codes, w_q_words, head, PASSES, 0, BLOCK)
+        load_scales(q0_planes, w_q_scales, head, PASSES, 0, BLOCK)
+        load_scales(q1_planes, w_q_scales, 0, PASSES, BLOCK, INNER)
+        load_codes(q1_codes, w_q_words, 0, PASSES, BLOCK, INNER)
+        load_scales(v_planes, w_v_scales, 0, PASSES, 0, INNER)
+        load_codes(v_codes, w_v_words, 0, head, 0, INNER)
+        load_codes(v_codes, w_v_words, head, PASSES, 0, INNER)
+        load_scales(k_planes, w_k_scales, 0, PASSES, 0, INNER)
+        load_codes(k_codes, w_k_words, 0, head, 0, INNER)
+        load_codes(k_codes, w_k_words, head, PASSES, 0, INNER)
+
+        nc.scalar.activation(out=table_seed[:], in_=table_seed[:], func=ACT.Abs_reciprocal_sqrt)
+
+        warm_bank = psum.tile([P, BLOCK], F32, tag="acc")
+        for w in range(WARM_UPS):
+            nc.tensor.matmul(out=warm_bank[:], lhsT=warm[:, 0:P], rhs=warm[:], start=True, stop=True)
+        gain_bank = psum.tile([P, 2 * DH], F32, tag="acc")
+        nc.tensor.matmul(out=gain_bank[:], lhsT=warm[:, 0:P], rhs=gain_rows[:], start=True, stop=True)
+
+        nc.vector.tensor_copy(out=gains[:].rearrange("p a d -> p (a d)"), in_=gain_bank[:])
+        pair_shape = [P, TOKEN_TILES * PAIRS, 2]
+        nc.vector.tensor_copy(
+            out=cos_pairs[:].rearrange("p t (i two) -> p (t i) two", two=2),
+            in_=cos_raw[:].rearrange("p t i -> p (t i)").unsqueeze(2).to_broadcast(pair_shape),
+        )
+        sin_split = sin_pairs[:].rearrange("p t (i two) -> p (t i) two", two=2)
+        sin_flat = sin_raw[:].rearrange("p t i -> p (t i)")
+        nc.vector.tensor_copy(out=sin_split[:, :, 0], in_=sin_flat)
+        nc.vector.tensor_scalar(out=sin_split[:, :, 1], in0=sin_flat, scalar1=-1.0, scalar2=None, op0=ALU.mult)
+        for a, (c_tab, s_tab) in enumerate(((q_cos, q_sin), (k_cos, k_sin))):
+            gain = gains[:, a, :].unsqueeze(1).to_broadcast([P, TOKEN_TILES, DH])
+            nc.vector.tensor_tensor(out=c_tab[:], in0=cos_pairs[:], in1=gain, op=ALU.mult)
+            nc.vector.tensor_tensor(out=s_tab[:], in0=sin_pairs[:], in1=gain, op=ALU.mult)
+
+        def mx_pass(acc, g, t, codes, planes, c0, width):
+            nc.tensor.matmul_mx(
+                out=acc[:],
+                lhsT=x_codes[:, g, 2 * P * t : 2 * P * (t + 1)].bitcast(FP4X4),
+                lhsT_scale=x_planes[:, g, P * t : P * (t + 1)],
+                rhs=codes[:, g, 2 * c0 : 2 * (c0 + width)].bitcast(FP4X4),
+                rhs_scale=planes[:, g, c0 : c0 + width],
+                start=(g == 0),
+                stop=(g == PASSES - 1),
+            )
+
+        tables = {"q": (q_cos, q_sin), "k": (k_cos, k_sin)}
+        to_add = []
+        to_scale = []
+
+        def finish_add():
+            if to_add:
+                t1, t2, rs, dst = to_add.pop(0)
+                summed = work.tile([P, BLOCK], F32)
+                swapped = t2[:].rearrange("p (i two) -> p i two", two=2)[:, :, ::-1]
+                nc.vector.tensor_tensor(
+                    out=summed[:].rearrange("p (i two) -> p i two", two=2),
+                    in0=t1[:].rearrange("p (i two) -> p i two", two=2),
+                    in1=swapped,
+                    op=ALU.add,
+                )
+                to_scale.append((summed, rs, dst))
+
+        def finish_scale():
+            if to_scale:
+                summed, rs, dst = to_scale.pop(0)
+                result = res.tile([P, BLOCK], F32)
+                for h in range(BLOCK_HEADS):
+                    cols = slice(h * DH, (h + 1) * DH)
+                    nc.scalar.activation(out=result[:, cols], in_=summed[:, cols], func=ACT.Copy, scale=rs[:, h : h + 1])
+                nc.sync.dma_start(out=dst, in_=result[:])
+
+        def norm_rope(acc, t, which, dst):
+            c_tab, s_tab = tables[which]
+            squares = work.tile([P, BLOCK], F32)
+            sums = work.tile([P, BLOCK_HEADS], F32)
+            rs = res.tile([P, BLOCK_HEADS], F32)
+            for h in range(BLOCK_HEADS):
+                cols = slice(h * DH, (h + 1) * DH)
+                nc.scalar.activation(out=squares[:, cols], in_=acc[:, cols], func=ACT.Square, accum_out=sums[:, h : h + 1])
+            nc.scalar.activation(out=rs[:], in_=sums[:], func=ACT.Abs_reciprocal_sqrt, scale=1.0 / DH, bias=EPS)
+            finish_scale()
+            t1 = work.tile([P, BLOCK], F32)
+            t2 = work.tile([P, BLOCK], F32)
+            heads = acc[:].rearrange("p (h d) -> p h d", h=BLOCK_HEADS)
+            shape = [P, BLOCK_HEADS, DH]
+            nc.vector.tensor_tensor(
+                out=t1[:].rearrange("p (h d) -> p h d", h=BLOCK_HEADS),
+                in0=heads, in1=c_tab[:, t, :].unsqueeze(1).to_broadcast(shape), op=ALU.mult,
+            )
+            finish_add()
+            nc.vector.tensor_tensor(
+                out=t2[:].rearrange("p (h d) -> p h d", h=BLOCK_HEADS),
+                in0=heads, in1=s_tab[:, t, :].unsqueeze(1).to_broadcast(shape), op=ALU.mult,
+            )
+            to_add.append((t1, t2, rs, dst))
+
+        def plain(acc, engine, width, dst):
+            copied = res.tile([P, BLOCK], F32)
+            if engine == "scalar":
+                nc.scalar.copy(out=copied[:, 0:width], in_=acc[:])
+            else:
+                nc.vector.tensor_copy(out=copied[:, 0:width], in_=acc[:])
+            finish_scale()
+            finish_add()
+            nc.sync.dma_start(out=dst, in_=copied[:, 0:width])
+
+        def rows(t):
+            return slice(P * t, P * (t + 1))
+
+        accs = []
+        for t in range(TOKEN_TILES):
+            acc = psum.tile([P, BLOCK], F32, tag="acc")
+            accs.append(acc)
+        for g in range(PASSES):
+            for t in range(TOKEN_TILES):
+                mx_pass(accs[t], g, t, q0_codes, q0_planes, 0, BLOCK)
+        for t in range(TOKEN_TILES):
+            norm_rope(accs[t], t, "q", outs["q"][rows(t), 0:BLOCK])
+
+        def block(which, codes, planes, c0, o0, engines):
+            for t in range(TOKEN_TILES):
+                widths = [BLOCK]
+                if which == "v" and o0 > 0 and t == TOKEN_TILES - 1:
+                    widths = [BLOCK // 2, BLOCK // 2]
+                at = 0
+                for piece, width in enumerate(widths):
+                    acc = psum.tile([P, width], F32, tag="acc")
+                    for g in range(PASSES):
+                        mx_pass(acc, g, t, codes, planes, c0 + at, width)
+                    dst = outs[which][rows(t), o0 + at : o0 + at + width]
+                    if which == "v":
+                        plain(acc, engines[t + piece], width, dst)
+                    else:
+                        norm_rope(acc, t, which, dst)
+                    at += width
+
+        block("q", q1_codes, q1_planes, 0, BLOCK, None)
+        block("v", v_codes, v_planes, 0, 0, ["scalar"] * 4)
+        block("k", k_codes, k_planes, 0, 0, None)
+        block("k", k_codes, k_planes, BLOCK, BLOCK, None)
+        block("v", v_codes, v_planes, BLOCK, BLOCK, ["scalar", "scalar", "vector", "scalar", "vector"])

@@ -21,8 +21,8 @@ PAIRS = DH // 2
 EPS = 1e-5
 FLOPS = 2 * TOKENS * D_IN * 3 * INNER
 
-HEAD_PASSES = 3
-WARM_UPS = 7
+HEAD_PASSES = 2
+WARM_UPS = 6
 
 
 def tile_flux2parallelselfattention_pa_kernel(
@@ -65,8 +65,10 @@ def tile_flux2parallelselfattention_pa_kernel(
         q1_planes = keep.tile([P, PASSES, BLOCK], U8, align_bytes=64)
         k_codes = keep.tile([P, PASSES, 2 * INNER], U8, align_bytes=64)
         k_planes = keep.tile([P, PASSES, INNER], U8, align_bytes=64)
-        v_codes = keep.tile([P, PASSES, 2 * INNER], U8, align_bytes=64)
-        v_planes = keep.tile([P, PASSES, INNER], U8, align_bytes=64)
+        v0_codes = keep.tile([P, PASSES, 2 * BLOCK], U8, align_bytes=64)
+        v0_planes = keep.tile([P, PASSES, BLOCK], U8, align_bytes=64)
+        v1_codes = keep.tile([P, PASSES, 2 * BLOCK], U8, align_bytes=64)
+        v1_planes = keep.tile([P, PASSES, BLOCK], U8, align_bytes=64)
         warm = keep.tile([P, BLOCK], BF16)
         gain_rows = keep.tile([P, 2 * DH], BF16)
         cos_raw = keep.tile([P, TOKEN_TILES, PAIRS], BF16)
@@ -97,63 +99,44 @@ def tile_flux2parallelselfattention_pa_kernel(
                 )
 
         head = HEAD_PASSES
-        zero(nc.vector, x_planes, 0, head)
+        zero(nc.vector, x_planes, 0, PASSES)
         zero(nc.gpsimd, q0_planes, 0, head)
         nc.vector.memset(warm[:], 1.0)
-        nc.gpsimd.memset(gain_rows[:], 0.0)
         nc.vector.memset(table_seed[:], 1.0)
-        zero(nc.vector, x_planes, head, PASSES)
+        nc.gpsimd.memset(gain_rows[:], 0.0)
+        zero(nc.vector, v0_planes, 0, PASSES)
         zero(nc.vector, q0_planes, head, PASSES)
-        zero(nc.vector, q1_planes, 0, PASSES)
 
         nc.gpsimd.dma_start(out=gain_rows[0:1, 0:DH], in_=norm_q_w.unsqueeze(0))
         nc.gpsimd.dma_start(out=gain_rows[0:1, DH : 2 * DH], in_=norm_k_w.unsqueeze(0))
+        zero(nc.gpsimd, q1_planes, 0, PASSES)
         nc.gpsimd.dma_start(out=cos_raw[:], in_=cos.rearrange("(t p) i -> p t i", p=P))
         nc.gpsimd.dma_start(out=sin_raw[:], in_=sin.rearrange("(t p) i -> p t i", p=P))
-        zero(nc.gpsimd, v_planes, 0, PASSES)
         zero(nc.gpsimd, k_planes, 0, PASSES)
+        zero(nc.gpsimd, v1_planes, 0, PASSES)
 
         load_codes(x_codes, hidden_words, 0, 1, 0, TOKENS)
         load_codes(q0_codes, w_q_words, 0, 1, 0, BLOCK)
-        load_scales(x_planes, hidden_scales, 0, head, 0, TOKENS)
+        load_scales(x_planes, hidden_scales, 0, PASSES, 0, TOKENS)
         load_scales(q0_planes, w_q_scales, 0, head, 0, BLOCK)
         load_codes(x_codes, hidden_words, 1, head, 0, TOKENS)
         load_codes(q0_codes, w_q_words, 1, head, 0, BLOCK)
-        load_scales(x_planes, hidden_scales, head, PASSES, 0, TOKENS)
+        load_codes(v0_codes, w_v_words, 0, head, 0, BLOCK)
+        load_scales(v0_planes, w_v_scales, 0, head, 0, BLOCK)
         load_codes(x_codes, hidden_words, head, PASSES, 0, TOKENS)
         load_codes(q0_codes, w_q_words, head, PASSES, 0, BLOCK)
         load_scales(q0_planes, w_q_scales, head, PASSES, 0, BLOCK)
+        load_codes(v0_codes, w_v_words, head, PASSES, 0, BLOCK)
+        load_scales(v0_planes, w_v_scales, head, PASSES, 0, BLOCK)
         load_scales(q1_planes, w_q_scales, 0, PASSES, BLOCK, INNER)
         load_codes(q1_codes, w_q_words, 0, PASSES, BLOCK, INNER)
-        load_scales(v_planes, w_v_scales, 0, PASSES, 0, INNER)
-        load_codes(v_codes, w_v_words, 0, head, 0, INNER)
-        load_codes(v_codes, w_v_words, head, PASSES, 0, INNER)
         load_scales(k_planes, w_k_scales, 0, PASSES, 0, INNER)
-        load_codes(k_codes, w_k_words, 0, head, 0, INNER)
-        load_codes(k_codes, w_k_words, head, PASSES, 0, INNER)
+        load_codes(k_codes, w_k_words, 0, 3, 0, INNER)
+        load_codes(k_codes, w_k_words, 3, PASSES, 0, INNER)
+        load_scales(v1_planes, w_v_scales, 0, PASSES, BLOCK, INNER)
+        load_codes(v1_codes, w_v_words, 0, PASSES, BLOCK, INNER)
 
         nc.scalar.activation(out=table_seed[:], in_=table_seed[:], func=ACT.Abs_reciprocal_sqrt)
-
-        warm_bank = psum.tile([P, BLOCK], F32, tag="acc")
-        for w in range(WARM_UPS):
-            nc.tensor.matmul(out=warm_bank[:], lhsT=warm[:, 0:P], rhs=warm[:], start=True, stop=True)
-        gain_bank = psum.tile([P, 2 * DH], F32, tag="acc")
-        nc.tensor.matmul(out=gain_bank[:], lhsT=warm[:, 0:P], rhs=gain_rows[:], start=True, stop=True)
-
-        nc.vector.tensor_copy(out=gains[:].rearrange("p a d -> p (a d)"), in_=gain_bank[:])
-        pair_shape = [P, TOKEN_TILES * PAIRS, 2]
-        nc.vector.tensor_copy(
-            out=cos_pairs[:].rearrange("p t (i two) -> p (t i) two", two=2),
-            in_=cos_raw[:].rearrange("p t i -> p (t i)").unsqueeze(2).to_broadcast(pair_shape),
-        )
-        sin_split = sin_pairs[:].rearrange("p t (i two) -> p (t i) two", two=2)
-        sin_flat = sin_raw[:].rearrange("p t i -> p (t i)")
-        nc.vector.tensor_copy(out=sin_split[:, :, 0], in_=sin_flat)
-        nc.vector.tensor_scalar(out=sin_split[:, :, 1], in0=sin_flat, scalar1=-1.0, scalar2=None, op0=ALU.mult)
-        for a, (c_tab, s_tab) in enumerate(((q_cos, q_sin), (k_cos, k_sin))):
-            gain = gains[:, a, :].unsqueeze(1).to_broadcast([P, TOKEN_TILES, DH])
-            nc.vector.tensor_tensor(out=c_tab[:], in0=cos_pairs[:], in1=gain, op=ALU.mult)
-            nc.vector.tensor_tensor(out=s_tab[:], in0=sin_pairs[:], in1=gain, op=ALU.mult)
 
         def mx_pass(acc, g, t, codes, planes, c0, width):
             nc.tensor.matmul_mx(
@@ -165,6 +148,40 @@ def tile_flux2parallelselfattention_pa_kernel(
                 start=(g == 0),
                 stop=(g == PASSES - 1),
             )
+
+        warm_bank = psum.tile([P, BLOCK], F32, tag="acc")
+        for w in range(WARM_UPS):
+            nc.tensor.matmul(out=warm_bank[:], lhsT=warm[:, 0:P], rhs=warm[:], start=True, stop=True)
+        gain_bank = psum.tile([P, 2 * DH], F32, tag="acc")
+
+        q0_accs = []
+        v0_accs = []
+        for t in range(TOKEN_TILES):
+            acc = psum.tile([P, BLOCK], F32, tag="acc")
+            q0_accs.append(acc)
+        for g in range(head):
+            for t in range(TOKEN_TILES):
+                mx_pass(q0_accs[t], g, t, q0_codes, q0_planes, 0, BLOCK)
+            if g == 0:
+                nc.tensor.matmul(out=gain_bank[:], lhsT=warm[:, 0:P], rhs=gain_rows[:], start=True, stop=True)
+
+        pair_shape = [P, TOKEN_TILES * PAIRS, 2]
+        nc.vector.tensor_copy(out=gains[:].rearrange("p a d -> p (a d)"), in_=gain_bank[:])
+        nc.vector.tensor_copy(
+            out=cos_pairs[:].rearrange("p t (i two) -> p (t i) two", two=2),
+            in_=cos_raw[:].rearrange("p t i -> p (t i)").unsqueeze(2).to_broadcast(pair_shape),
+        )
+        sin_split = sin_pairs[:].rearrange("p t (i two) -> p (t i) two", two=2)
+        sin_flat = sin_raw[:].rearrange("p t i -> p (t i)")
+        nc.vector.tensor_copy(out=sin_split[:, :, 0], in_=sin_flat)
+        nc.vector.tensor_scalar(out=sin_split[:, :, 1], in0=sin_flat, scalar1=-1.0, scalar2=None, op0=ALU.mult)
+
+        def build_tables(which, c_tab, s_tab):
+            gain = gains[:, which, :].unsqueeze(1).to_broadcast([P, TOKEN_TILES, DH])
+            nc.vector.tensor_tensor(out=c_tab[:], in0=cos_pairs[:], in1=gain, op=ALU.mult)
+            nc.vector.tensor_tensor(out=s_tab[:], in0=sin_pairs[:], in1=gain, op=ALU.mult)
+
+        build_tables(0, q_cos, q_sin)
 
         tables = {"q": (q_cos, q_sin), "k": (k_cos, k_sin)}
         to_add = []
@@ -230,21 +247,27 @@ def tile_flux2parallelselfattention_pa_kernel(
         def rows(t):
             return slice(P * t, P * (t + 1))
 
-        accs = []
         for t in range(TOKEN_TILES):
             acc = psum.tile([P, BLOCK], F32, tag="acc")
-            accs.append(acc)
-        for g in range(PASSES):
+            v0_accs.append(acc)
+        for g in range(head):
             for t in range(TOKEN_TILES):
-                mx_pass(accs[t], g, t, q0_codes, q0_planes, 0, BLOCK)
+                mx_pass(v0_accs[t], g, t, v0_codes, v0_planes, 0, BLOCK)
         for t in range(TOKEN_TILES):
-            norm_rope(accs[t], t, "q", outs["q"][rows(t), 0:BLOCK])
+            for g in range(head, PASSES):
+                mx_pass(q0_accs[t], g, t, q0_codes, q0_planes, 0, BLOCK)
+            norm_rope(q0_accs[t], t, "q", outs["q"][rows(t), 0:BLOCK])
+        for t in range(TOKEN_TILES):
+            for g in range(head, PASSES):
+                mx_pass(v0_accs[t], g, t, v0_codes, v0_planes, 0, BLOCK)
+            plain(v0_accs[t], "scalar", BLOCK, outs["v"][rows(t), 0:BLOCK])
+        build_tables(1, k_cos, k_sin)
 
         def block(which, codes, planes, c0, o0, engines):
             for t in range(TOKEN_TILES):
                 widths = [BLOCK]
                 if which == "v" and o0 > 0 and t == TOKEN_TILES - 1:
-                    widths = [BLOCK // 2, BLOCK // 2]
+                    widths = [BLOCK // 2, BLOCK // 4, BLOCK // 4]
                 at = 0
                 for piece, width in enumerate(widths):
                     acc = psum.tile([P, width], F32, tag="acc")
@@ -258,7 +281,6 @@ def tile_flux2parallelselfattention_pa_kernel(
                     at += width
 
         block("q", q1_codes, q1_planes, 0, BLOCK, None)
-        block("v", v_codes, v_planes, 0, 0, ["scalar"] * 4)
         block("k", k_codes, k_planes, 0, 0, None)
         block("k", k_codes, k_planes, BLOCK, BLOCK, None)
-        block("v", v_codes, v_planes, BLOCK, BLOCK, ["scalar", "scalar", "vector", "scalar", "vector"])
+        block("v", v1_codes, v1_planes, 0, BLOCK, ["scalar", "scalar", "vector", "scalar", "vector", "scalar"])

@@ -53,22 +53,27 @@ def tile_flux2parallelselfattention_pa_kernel(
     with ExitStack() as ctx:
         keep = ctx.enter_context(tc.tile_pool(name="keep", bufs=1))
         work = ctx.enter_context(tc.tile_pool(name="work", bufs=3))
+        late = ctx.enter_context(tc.tile_pool(name="late", bufs=7))
         res = ctx.enter_context(tc.tile_pool(name="res", bufs=6))
         psum = ctx.enter_context(tc.psum_pool(name="psum", bufs=8))
         ctx.enter_context(tc.manual_schedule())
 
         x_codes = keep.tile([P, PASSES, 2 * TOKENS], U8, align_bytes=64)
-        x_planes = keep.tile([P, PASSES, TOKENS], U8, align_bytes=64)
+        x_planes_all = keep.tile([P, PASSES, TOKENS], U8, align_bytes=64)
+        x_planes = [x_planes_all]
         q0_codes = keep.tile([P, PASSES, 2 * BLOCK], U8, align_bytes=64)
-        q0_planes = keep.tile([P, PASSES, BLOCK], U8, align_bytes=64)
+        q0_planes_a = keep.tile([P, HEAD_PASSES, BLOCK], U8, align_bytes=64)
+        q0_planes_b = keep.tile([P, PASSES - HEAD_PASSES, BLOCK], U8, align_bytes=64)
+        q0_planes = [q0_planes_a, q0_planes_b]
         q1_codes = keep.tile([P, PASSES, 2 * BLOCK], U8, align_bytes=64)
-        q1_planes = keep.tile([P, PASSES, BLOCK], U8, align_bytes=64)
+        q1_planes_all = keep.tile([P, PASSES, BLOCK], U8, align_bytes=64)
+        q1_planes = [q1_planes_all]
         k_codes = keep.tile([P, PASSES, 2 * INNER], U8, align_bytes=64)
-        k_planes = keep.tile([P, PASSES, INNER], U8, align_bytes=64)
-        v0_codes = keep.tile([P, PASSES, 2 * BLOCK], U8, align_bytes=64)
-        v0_planes = keep.tile([P, PASSES, BLOCK], U8, align_bytes=64)
-        v1_codes = keep.tile([P, PASSES, 2 * BLOCK], U8, align_bytes=64)
-        v1_planes = keep.tile([P, PASSES, BLOCK], U8, align_bytes=64)
+        k_planes_all = keep.tile([P, PASSES, INNER], U8, align_bytes=64)
+        k_planes = [k_planes_all]
+        v_codes = keep.tile([P, PASSES, 2 * INNER], U8, align_bytes=64)
+        v_planes_all = keep.tile([P, PASSES, INNER], U8, align_bytes=64)
+        v_planes = [v_planes_all]
         warm = keep.tile([P, BLOCK], BF16)
         gain_rows = keep.tile([P, 2 * DH], BF16)
         cos_raw = keep.tile([P, TOKEN_TILES, PAIRS], BF16)
@@ -82,8 +87,14 @@ def tile_flux2parallelselfattention_pa_kernel(
         k_sin = keep.tile([P, TOKEN_TILES, DH], F32)
         table_seed = keep.tile([P, 1], F32)
 
-        def zero(engine, planes, g0, g1):
-            engine.memset(planes[:, g0:g1, :].bitcast(I32), 0)
+        def zero(engine, planes):
+            engine.memset(planes[:].bitcast(I32), 0)
+
+        def plane_of(planes, g):
+            for tile in planes:
+                if g < tile.shape[1]:
+                    return tile[:, g, :]
+                g -= tile.shape[1]
 
         def load_codes(tile, words, g0, g1, c0, c1):
             nc.sync.dma_start(
@@ -91,50 +102,48 @@ def tile_flux2parallelselfattention_pa_kernel(
                 in_=words[g0:g1, :, 2 * c0 : 2 * c1].rearrange("g p n -> p g n"),
             )
 
-        def load_scales(planes, scales, g0, g1, c0, c1):
-            for quad in range(4):
+        def load_scales(planes, scales, g0, c0, c1):
+            g1 = g0 + planes.shape[1]
+            for r in range(4):
                 nc.sync.dma_start(
-                    out=planes[32 * quad : 32 * quad + 4, g0:g1, :].bitcast(I32),
-                    in_=scales[g0:g1, 4 * quad : 4 * quad + 4, c0:c1].rearrange("g r n -> r g n").bitcast(I32),
+                    out=planes[r:P:32, :, :].bitcast(I32),
+                    in_=scales[g0:g1, r:16:4, c0:c1].rearrange("g q n -> q g n").bitcast(I32),
                 )
 
         head = HEAD_PASSES
-        zero(nc.vector, x_planes, 0, PASSES)
-        zero(nc.gpsimd, q0_planes, 0, head)
+        zero(nc.vector, x_planes_all)
+        zero(nc.gpsimd, q0_planes_a)
         nc.vector.memset(warm[:], 1.0)
         nc.vector.memset(table_seed[:], 1.0)
         nc.gpsimd.memset(gain_rows[:], 0.0)
-        zero(nc.vector, v0_planes, 0, PASSES)
-        zero(nc.vector, q0_planes, head, PASSES)
+        zero(nc.vector, q1_planes_all)
+        zero(nc.vector, q0_planes_b)
 
         nc.gpsimd.dma_start(out=gain_rows[0:1, 0:DH], in_=norm_q_w.unsqueeze(0))
         nc.gpsimd.dma_start(out=gain_rows[0:1, DH : 2 * DH], in_=norm_k_w.unsqueeze(0))
-        zero(nc.gpsimd, q1_planes, 0, PASSES)
         nc.gpsimd.dma_start(out=cos_raw[:], in_=cos.rearrange("(t p) i -> p t i", p=P))
         nc.gpsimd.dma_start(out=sin_raw[:], in_=sin.rearrange("(t p) i -> p t i", p=P))
-        zero(nc.gpsimd, k_planes, 0, PASSES)
-        zero(nc.gpsimd, v1_planes, 0, PASSES)
+        zero(nc.gpsimd, k_planes_all)
+        zero(nc.gpsimd, v_planes_all)
 
         load_codes(x_codes, hidden_words, 0, 1, 0, TOKENS)
         load_codes(q0_codes, w_q_words, 0, 1, 0, BLOCK)
-        load_scales(x_planes, hidden_scales, 0, PASSES, 0, TOKENS)
-        load_scales(q0_planes, w_q_scales, 0, head, 0, BLOCK)
+        load_scales(x_planes_all, hidden_scales, 0, 0, TOKENS)
+        load_scales(q0_planes_a, w_q_scales, 0, 0, BLOCK)
         load_codes(x_codes, hidden_words, 1, head, 0, TOKENS)
         load_codes(q0_codes, w_q_words, 1, head, 0, BLOCK)
-        load_codes(v0_codes, w_v_words, 0, head, 0, BLOCK)
-        load_scales(v0_planes, w_v_scales, 0, head, 0, BLOCK)
+        load_codes(q1_codes, w_q_words, 0, head, BLOCK, INNER)
+        load_scales(q1_planes_all, w_q_scales, 0, BLOCK, INNER)
         load_codes(x_codes, hidden_words, head, PASSES, 0, TOKENS)
         load_codes(q0_codes, w_q_words, head, PASSES, 0, BLOCK)
-        load_scales(q0_planes, w_q_scales, head, PASSES, 0, BLOCK)
-        load_codes(v0_codes, w_v_words, head, PASSES, 0, BLOCK)
-        load_scales(v0_planes, w_v_scales, head, PASSES, 0, BLOCK)
-        load_scales(q1_planes, w_q_scales, 0, PASSES, BLOCK, INNER)
-        load_codes(q1_codes, w_q_words, 0, PASSES, BLOCK, INNER)
-        load_scales(k_planes, w_k_scales, 0, PASSES, 0, INNER)
+        load_scales(q0_planes_b, w_q_scales, head, 0, BLOCK)
+        load_codes(q1_codes, w_q_words, head, PASSES, BLOCK, INNER)
+        load_scales(k_planes_all, w_k_scales, 0, 0, INNER)
         load_codes(k_codes, w_k_words, 0, 3, 0, INNER)
         load_codes(k_codes, w_k_words, 3, PASSES, 0, INNER)
-        load_scales(v1_planes, w_v_scales, 0, PASSES, BLOCK, INNER)
-        load_codes(v1_codes, w_v_words, 0, PASSES, BLOCK, INNER)
+        load_scales(v_planes_all, w_v_scales, 0, 0, INNER)
+        load_codes(v_codes, w_v_words, 0, 3, 0, INNER)
+        load_codes(v_codes, w_v_words, 3, PASSES, 0, INNER)
 
         nc.scalar.activation(out=table_seed[:], in_=table_seed[:], func=ACT.Abs_reciprocal_sqrt)
 
@@ -142,9 +151,9 @@ def tile_flux2parallelselfattention_pa_kernel(
             nc.tensor.matmul_mx(
                 out=acc[:],
                 lhsT=x_codes[:, g, 2 * P * t : 2 * P * (t + 1)].bitcast(FP4X4),
-                lhsT_scale=x_planes[:, g, P * t : P * (t + 1)],
+                lhsT_scale=plane_of(x_planes, g)[:, P * t : P * (t + 1)],
                 rhs=codes[:, g, 2 * c0 : 2 * (c0 + width)].bitcast(FP4X4),
-                rhs_scale=planes[:, g, c0 : c0 + width],
+                rhs_scale=plane_of(planes, g)[:, c0 : c0 + width],
                 start=(g == 0),
                 stop=(g == PASSES - 1),
             )
@@ -155,7 +164,7 @@ def tile_flux2parallelselfattention_pa_kernel(
         gain_bank = psum.tile([P, 2 * DH], F32, tag="acc")
 
         q0_accs = []
-        v0_accs = []
+        q1_accs = []
         for t in range(TOKEN_TILES):
             acc = psum.tile([P, BLOCK], F32, tag="acc")
             q0_accs.append(acc)
@@ -182,6 +191,7 @@ def tile_flux2parallelselfattention_pa_kernel(
             nc.vector.tensor_tensor(out=s_tab[:], in0=sin_pairs[:], in1=gain, op=ALU.mult)
 
         build_tables(0, q_cos, q_sin)
+        build_tables(1, k_cos, k_sin)
 
         tables = {"q": (q_cos, q_sin), "k": (k_cos, k_sin)}
         to_add = []
@@ -190,7 +200,7 @@ def tile_flux2parallelselfattention_pa_kernel(
         def finish_add():
             if to_add:
                 t1, t2, rs, dst = to_add.pop(0)
-                summed = work.tile([P, BLOCK], F32)
+                summed = late.tile([P, BLOCK], F32)
                 swapped = t2[:].rearrange("p (i two) -> p i two", two=2)[:, :, ::-1]
                 nc.vector.tensor_tensor(
                     out=summed[:].rearrange("p (i two) -> p i two", two=2),
@@ -200,8 +210,8 @@ def tile_flux2parallelselfattention_pa_kernel(
                 )
                 to_scale.append((summed, rs, dst))
 
-        def finish_scale():
-            if to_scale:
+        def finish_scale(keep_back):
+            if len(to_scale) > keep_back:
                 summed, rs, dst = to_scale.pop(0)
                 result = res.tile([P, BLOCK], F32)
                 for h in range(BLOCK_HEADS):
@@ -209,16 +219,16 @@ def tile_flux2parallelselfattention_pa_kernel(
                     nc.scalar.activation(out=result[:, cols], in_=summed[:, cols], func=ACT.Copy, scale=rs[:, h : h + 1])
                 nc.sync.dma_start(out=dst, in_=result[:])
 
-        def norm_rope(acc, t, which, dst):
+        def norm_rope(acc, t, which, dst, keep_back):
             c_tab, s_tab = tables[which]
             squares = work.tile([P, BLOCK], F32)
             sums = work.tile([P, BLOCK_HEADS], F32)
-            rs = res.tile([P, BLOCK_HEADS], F32)
+            rs = late.tile([P, BLOCK_HEADS], F32)
             for h in range(BLOCK_HEADS):
                 cols = slice(h * DH, (h + 1) * DH)
                 nc.scalar.activation(out=squares[:, cols], in_=acc[:, cols], func=ACT.Square, accum_out=sums[:, h : h + 1])
             nc.scalar.activation(out=rs[:], in_=sums[:], func=ACT.Abs_reciprocal_sqrt, scale=1.0 / DH, bias=EPS)
-            finish_scale()
+            finish_scale(keep_back)
             t1 = work.tile([P, BLOCK], F32)
             t2 = work.tile([P, BLOCK], F32)
             heads = acc[:].rearrange("p (h d) -> p h d", h=BLOCK_HEADS)
@@ -234,53 +244,52 @@ def tile_flux2parallelselfattention_pa_kernel(
             )
             to_add.append((t1, t2, rs, dst))
 
-        def plain(acc, engine, width, dst):
+        def plain(acc, engine, width, dst, keep_back):
             copied = res.tile([P, BLOCK], F32)
             if engine == "scalar":
                 nc.scalar.copy(out=copied[:, 0:width], in_=acc[:])
             else:
                 nc.vector.tensor_copy(out=copied[:, 0:width], in_=acc[:])
-            finish_scale()
-            finish_add()
             nc.sync.dma_start(out=dst, in_=copied[:, 0:width])
+            finish_add()
+            finish_scale(keep_back)
 
         def rows(t):
             return slice(P * t, P * (t + 1))
 
         for t in range(TOKEN_TILES):
             acc = psum.tile([P, BLOCK], F32, tag="acc")
-            v0_accs.append(acc)
+            q1_accs.append(acc)
         for g in range(head):
             for t in range(TOKEN_TILES):
-                mx_pass(v0_accs[t], g, t, v0_codes, v0_planes, 0, BLOCK)
-        for t in range(TOKEN_TILES):
-            for g in range(head, PASSES):
-                mx_pass(q0_accs[t], g, t, q0_codes, q0_planes, 0, BLOCK)
-            norm_rope(q0_accs[t], t, "q", outs["q"][rows(t), 0:BLOCK])
-        for t in range(TOKEN_TILES):
-            for g in range(head, PASSES):
-                mx_pass(v0_accs[t], g, t, v0_codes, v0_planes, 0, BLOCK)
-            plain(v0_accs[t], "scalar", BLOCK, outs["v"][rows(t), 0:BLOCK])
-        build_tables(1, k_cos, k_sin)
-
-        def block(which, codes, planes, c0, o0, engines):
+                mx_pass(q1_accs[t], g, t, q1_codes, q1_planes, 0, BLOCK)
+        for accs, codes, planes, o0 in ((q0_accs, q0_codes, q0_planes, 0), (q1_accs, q1_codes, q1_planes, BLOCK)):
             for t in range(TOKEN_TILES):
-                widths = [BLOCK]
-                if which == "v" and o0 > 0 and t == TOKEN_TILES - 1:
-                    widths = [BLOCK // 2, BLOCK // 4, BLOCK // 4]
-                at = 0
-                for piece, width in enumerate(widths):
-                    acc = psum.tile([P, width], F32, tag="acc")
-                    for g in range(PASSES):
-                        mx_pass(acc, g, t, codes, planes, c0 + at, width)
-                    dst = outs[which][rows(t), o0 + at : o0 + at + width]
-                    if which == "v":
-                        plain(acc, engines[t + piece], width, dst)
-                    else:
-                        norm_rope(acc, t, which, dst)
-                    at += width
+                for g in range(head, PASSES):
+                    mx_pass(accs[t], g, t, codes, planes, 0, BLOCK)
+                norm_rope(accs[t], t, "q", outs["q"][rows(t), o0 : o0 + BLOCK], 0)
 
-        block("q", q1_codes, q1_planes, 0, BLOCK, None)
-        block("k", k_codes, k_planes, 0, 0, None)
-        block("k", k_codes, k_planes, BLOCK, BLOCK, None)
-        block("v", v1_codes, v1_planes, 0, BLOCK, ["scalar", "scalar", "vector", "scalar", "vector", "scalar"])
+        def product(codes, planes, t, c0, width):
+            acc = psum.tile([P, width], F32, tag="acc")
+            for g in range(PASSES):
+                mx_pass(acc, g, t, codes, planes, c0, width)
+            return acc
+
+        for half in range(2):
+            for t in range(TOKEN_TILES):
+                acc = product(k_codes, k_planes, t, half * BLOCK, BLOCK)
+                norm_rope(acc, t, "k", outs["k"][rows(t), half * BLOCK : (half + 1) * BLOCK], 1 + half)
+
+        for t in range(TOKEN_TILES):
+            acc = product(v_codes, v_planes, t, 0, BLOCK)
+            plain(acc, "scalar", BLOCK, outs["v"][rows(t), 0:BLOCK], 3 if t == 0 else 0)
+        for t, c0, width, engine in (
+            (0, 512, 512, "scalar"),
+            (1, 512, 512, "scalar"),
+            (2, 512, 512, "vector"),
+            (3, 512, 256, "scalar"),
+            (3, 768, 128, "vector"),
+            (3, 896, 128, "scalar"),
+        ):
+            acc = product(v_codes, v_planes, t, c0, width)
+            plain(acc, engine, width, outs["v"][rows(t), c0 : c0 + width], 0)

@@ -116,14 +116,14 @@ def tile_flux2parallelselfattention_pa_kernel(
         nc.vector.memset(warm[:], 1.0)
         nc.vector.memset(table_seed[:], 1.0)
         nc.gpsimd.memset(gain_rows[:], 0.0)
-        zero(nc.vector, q1_planes_all)
         zero(nc.vector, q0_planes_b)
+        zero(nc.vector, k_planes_all)
 
         nc.gpsimd.dma_start(out=gain_rows[0:1, 0:DH], in_=norm_q_w.unsqueeze(0))
         nc.gpsimd.dma_start(out=gain_rows[0:1, DH : 2 * DH], in_=norm_k_w.unsqueeze(0))
+        zero(nc.gpsimd, q1_planes_all)
         nc.gpsimd.dma_start(out=cos_raw[:], in_=cos.rearrange("(t p) i -> p t i", p=P))
         nc.gpsimd.dma_start(out=sin_raw[:], in_=sin.rearrange("(t p) i -> p t i", p=P))
-        zero(nc.gpsimd, k_planes_all)
         zero(nc.gpsimd, v_planes_all)
 
         load_codes(x_codes, hidden_words, 0, 1, 0, TOKENS)
@@ -134,9 +134,11 @@ def tile_flux2parallelselfattention_pa_kernel(
         load_codes(q0_codes, w_q_words, 1, head, 0, BLOCK)
         load_codes(q1_codes, w_q_words, 0, head, BLOCK, INNER)
         load_scales(q1_planes_all, w_q_scales, 0, BLOCK, INNER)
-        load_codes(x_codes, hidden_words, head, PASSES, 0, TOKENS)
-        load_codes(q0_codes, w_q_words, head, PASSES, 0, BLOCK)
+        load_codes(x_codes, hidden_words, head, 4, 0, TOKENS)
+        load_codes(q0_codes, w_q_words, head, 4, 0, BLOCK)
         load_scales(q0_planes_b, w_q_scales, head, 0, BLOCK)
+        load_codes(x_codes, hidden_words, 4, PASSES, 0, TOKENS)
+        load_codes(q0_codes, w_q_words, 4, PASSES, 0, BLOCK)
         load_codes(q1_codes, w_q_words, head, PASSES, BLOCK, INNER)
         load_scales(k_planes_all, w_k_scales, 0, 0, INNER)
         load_codes(k_codes, w_k_words, 0, 3, 0, INNER)
@@ -263,9 +265,12 @@ def tile_flux2parallelselfattention_pa_kernel(
         for g in range(head):
             for t in range(TOKEN_TILES):
                 mx_pass(q1_accs[t], g, t, q1_codes, q1_planes, 0, BLOCK)
+        for t in range(TOKEN_TILES):
+            for g in range(head, 4):
+                mx_pass(q0_accs[t], g, t, q0_codes, q0_planes, 0, BLOCK)
         for accs, codes, planes, o0 in ((q0_accs, q0_codes, q0_planes, 0), (q1_accs, q1_codes, q1_planes, BLOCK)):
             for t in range(TOKEN_TILES):
-                for g in range(head, PASSES):
+                for g in range(4 if o0 == 0 else head, PASSES):
                     mx_pass(accs[t], g, t, codes, planes, 0, BLOCK)
                 norm_rope(accs[t], t, "q", outs["q"][rows(t), o0 : o0 + BLOCK], 0)
 

from contextlib import ExitStack

import concourse.mybir as mybir

F32 = mybir.dt.float32
BF16 = mybir.dt.bfloat16
U8 = mybir.dt.uint8
I32 = mybir.dt.int32
FP4X4 = mybir.dt.float4_e2m1fn_x4
ACT = mybir.ActivationFunctionType
ALU = mybir.AluOpType

P = 128
TOKENS, D_IN, HEADS, DH = 512, 3072, 8, 128
INNER = HEADS * DH
PASSES = D_IN // 512
TOKEN_TILES = TOKENS // P
BLOCK = 512
BLOCK_HEADS = BLOCK // DH
PAIRS = DH // 2
EPS = 1e-5
FLOPS = 2 * TOKENS * D_IN * 3 * INNER

HEAD_PASSES = 2
WARM_UPS = 6


def tile_flux2parallelselfattention_pa_kernel(
    tc,
    hidden_words,
    hidden_scales,
    w_q_words,
    w_q_scales,
    w_k_words,
    w_k_scales,
    w_v_words,
    w_v_scales,
    norm_q_w,
    norm_k_w,
    cos,
    sin,
    out_q,
    out_k,
    out_v,
):
    nc = tc.nc
    outs = {
        "q": out_q.rearrange("b s h d -> (b s) (h d)"),
        "k": out_k.rearrange("b s h d -> (b s) (h d)"),
        "v": out_v.rearrange("b s h d -> (b s) (h d)"),
    }

    with ExitStack() as ctx:
        keep = ctx.enter_context(tc.tile_pool(name="keep", bufs=1))
        work = ctx.enter_context(tc.tile_pool(name="work", bufs=3))
        late = ctx.enter_context(tc.tile_pool(name="late", bufs=7))
        res = ctx.enter_context(tc.tile_pool(name="res", bufs=6))
        psum = ctx.enter_context(tc.psum_pool(name="psum", bufs=8))
        ctx.enter_context(tc.manual_schedule())

        x_codes = keep.tile([P, PASSES, 2 * TOKENS], U8, align_bytes=64)
        x_planes_all = keep.tile([P, PASSES, TOKENS], U8, align_bytes=64)
        x_planes = [x_planes_all]
        q0_codes = keep.tile([P, PASSES, 2 * BLOCK], U8, align_bytes=64)
        q0_planes_a = keep.tile([P, HEAD_PASSES, BLOCK], U8, align_bytes=64)
        q0_planes_b = keep.tile([P, PASSES - HEAD_PASSES, BLOCK], U8, align_bytes=64)
        q0_planes = [q0_planes_a, q0_planes_b]
        q1_codes = keep.tile([P, PASSES, 2 * BLOCK], U8, align_bytes=64)
        q1_planes_all = keep.tile([P, PASSES, BLOCK], U8, align_bytes=64)
        q1_planes = [q1_planes_all]
        k_codes = keep.tile([P, PASSES, 2 * INNER], U8, align_bytes=64)
        k_planes_all = keep.tile([P, PASSES, INNER], U8, align_bytes=64)
        k_planes = [k_planes_all]
        v_codes = keep.tile([P, PASSES, 2 * INNER], U8, align_bytes=64)
        v_planes_all = keep.tile([P, PASSES, INNER], U8, align_bytes=64)
        v_planes = [v_planes_all]
        warm = keep.tile([P, BLOCK], BF16)
        gain_rows = keep.tile([P, 2 * DH], BF16)
        cos_raw = keep.tile([P, TOKEN_TILES, PAIRS], BF16)
        sin_raw = keep.tile([P, TOKEN_TILES, PAIRS], BF16)
        gains = keep.tile([P, 2, DH], F32)
        cos_pairs = keep.tile([P, TOKEN_TILES, DH], F32)
        sin_pairs = keep.tile([P, TOKEN_TILES, DH], F32)
        q_cos = keep.tile([P, TOKEN_TILES, DH], F32)
        q_sin = keep.tile([P, TOKEN_TILES, DH], F32)
        k_cos = keep.tile([P, TOKEN_TILES, DH], F32)
        k_sin = keep.tile([P, TOKEN_TILES, DH], F32)
        table_seed = keep.tile([P, 1], F32)

        def zero(engine, planes):
            engine.memset(planes[:].bitcast(I32), 0)

        def plane_of(planes, g):
            for tile in planes:
                if g < tile.shape[1]:
                    return tile[:, g, :]
                g -= tile.shape[1]

        def load_codes(tile, words, g0, g1, c0, c1):
            nc.sync.dma_start(
                out=tile[:, g0:g1, :],
                in_=words[g0:g1, :, 2 * c0 : 2 * c1].rearrange("g p n -> p g n"),
            )

        def load_scales(planes, scales, g0, c0, c1):
            g1 = g0 + planes.shape[1]
            for r in range(4):
                nc.sync.dma_start(
                    out=planes[r:P:32, :, :].bitcast(I32),
                    in_=scales[g0:g1, r:16:4, c0:c1].rearrange("g q n -> q g n").bitcast(I32),
                )

        head = HEAD_PASSES
        zero(nc.vector, x_planes_all)
        zero(nc.gpsimd, q0_planes_a)
        nc.vector.memset(warm[:], 1.0)
        nc.vector.memset(table_seed[:], 1.0)
        nc.gpsimd.memset(gain_rows[:], 0.0)
        zero(nc.vector, q0_planes_b)
        zero(nc.vector, k_planes_all)

        nc.gpsimd.dma_start(out=gain_rows[0:1, 0:DH], in_=norm_q_w.unsqueeze(0))
        nc.gpsimd.dma_start(out=gain_rows[0:1, DH : 2 * DH], in_=norm_k_w.unsqueeze(0))
        zero(nc.gpsimd, q1_planes_all)
        nc.gpsimd.dma_start(out=cos_raw[:], in_=cos.rearrange("(t p) i -> p t i", p=P))
        nc.gpsimd.dma_start(out=sin_raw[:], in_=sin.rearrange("(t p) i -> p t i", p=P))
        zero(nc.gpsimd, v_planes_all)

        load_codes(x_codes, hidden_words, 0, 1, 0, TOKENS)
        load_codes(q0_codes, w_q_words, 0, 1, 0, BLOCK)
        load_scales(x_planes_all, hidden_scales, 0, 0, TOKENS)
        load_scales(q0_planes_a, w_q_scales, 0, 0, BLOCK)
        load_codes(x_codes, hidden_words, 1, head, 0, TOKENS)
        load_codes(q0_codes, w_q_words, 1, head, 0, BLOCK)
        load_codes(q1_codes, w_q_words, 0, head, BLOCK, INNER)
        load_scales(q1_planes_all, w_q_scales, 0, BLOCK, INNER)
        load_codes(x_codes, hidden_words, head, 4, 0, TOKENS)
        load_codes(q0_codes, w_q_words, head, 4, 0, BLOCK)
        load_scales(q0_planes_b, w_q_scales, head, 0, BLOCK)
        load_codes(x_codes, hidden_words, 4, PASSES, 0, TOKENS)
        load_codes(q0_codes, w_q_words, 4, PASSES, 0, BLOCK)
        load_codes(q1_codes, w_q_words, head, PASSES, BLOCK, INNER)
        load_scales(k_planes_all, w_k_scales, 0, 0, INNER)
        load_codes(k_codes, w_k_words, 0, 3, 0, INNER)
        load_codes(k_codes, w_k_words, 3, PASSES, 0, INNER)
        load_scales(v_planes_all, w_v_scales, 0, 0, INNER)
        load_codes(v_codes, w_v_words, 0, 3, 0, INNER)
        load_codes(v_codes, w_v_words, 3, PASSES, 0, INNER)

        nc.scalar.activation(out=table_seed[:], in_=table_seed[:], func=ACT.Abs_reciprocal_sqrt)

        def mx_pass(acc, g, t, codes, planes, c0, width):
            nc.tensor.matmul_mx(
                out=acc[:],
                lhsT=x_codes[:, g, 2 * P * t : 2 * P * (t + 1)].bitcast(FP4X4),
                lhsT_scale=plane_of(x_planes, g)[:, P * t : P * (t + 1)],
                rhs=codes[:, g, 2 * c0 : 2 * (c0 + width)].bitcast(FP4X4),
                rhs_scale=plane_of(planes, g)[:, c0 : c0 + width],
                start=(g == 0),
                stop=(g == PASSES - 1),
            )

        warm_bank = psum.tile([P, BLOCK], F32, tag="acc")
        for w in range(WARM_UPS):
            nc.tensor.matmul(out=warm_bank[:], lhsT=warm[:, 0:P], rhs=warm[:], start=True, stop=True)
        gain_bank = psum.tile([P, 2 * DH], F32, tag="acc")

        q0_accs = []
        q1_accs = []
        for t in range(TOKEN_TILES):
            acc = psum.tile([P, BLOCK], F32, tag="acc")
            q0_accs.append(acc)
        for g in range(head):
            for t in range(TOKEN_TILES):
                mx_pass(q0_accs[t], g, t, q0_codes, q0_planes, 0, BLOCK)
            if g == 0:
                nc.tensor.matmul(out=gain_bank[:], lhsT=warm[:, 0:P], rhs=gain_rows[:], start=True, stop=True)

        pair_shape = [P, TOKEN_TILES * PAIRS, 2]
        nc.vector.tensor_copy(out=gains[:].rearrange("p a d -> p (a d)"), in_=gain_bank[:])
        nc.vector.tensor_copy(
            out=cos_pairs[:].rearrange("p t (i two) -> p (t i) two", two=2),
            in_=cos_raw[:].rearrange("p t i -> p (t i)").unsqueeze(2).to_broadcast(pair_shape),
        )
        sin_split = sin_pairs[:].rearrange("p t (i two) -> p (t i) two", two=2)
        sin_flat = sin_raw[:].rearrange("p t i -> p (t i)")
        nc.vector.tensor_copy(out=sin_split[:, :, 0], in_=sin_flat)
        nc.vector.tensor_scalar(out=sin_split[:, :, 1], in0=sin_flat, scalar1=-1.0, scalar2=None, op0=ALU.mult)

        def build_tables(which, c_tab, s_tab):
            gain = gains[:, which, :].unsqueeze(1).to_broadcast([P, TOKEN_TILES, DH])
            nc.vector.tensor_tensor(out=c_tab[:], in0=cos_pairs[:], in1=gain, op=ALU.mult)
            nc.vector.tensor_tensor(out=s_tab[:], in0=sin_pairs[:], in1=gain, op=ALU.mult)

        build_tables(0, q_cos, q_sin)
        build_tables(1, k_cos, k_sin)

        tables = {"q": (q_cos, q_sin), "k": (k_cos, k_sin)}
        to_add = []
        to_scale = []

        def finish_add():
            if to_add:
                t1, t2, rs, dst = to_add.pop(0)
                summed = late.tile([P, BLOCK], F32)
                swapped = t2[:].rearrange("p (i two) -> p i two", two=2)[:, :, ::-1]
                nc.vector.tensor_tensor(
                    out=summed[:].rearrange("p (i two) -> p i two", two=2),
                    in0=t1[:].rearrange("p (i two) -> p i two", two=2),
                    in1=swapped,
                    op=ALU.add,
                )
                to_scale.append((summed, rs, dst))

        def finish_scale(keep_back):
            if len(to_scale) > keep_back:
                summed, rs, dst = to_scale.pop(0)
                result = res.tile([P, BLOCK], F32)
                for h in range(BLOCK_HEADS):
                    cols = slice(h * DH, (h + 1) * DH)
                    nc.scalar.activation(out=result[:, cols], in_=summed[:, cols], func=ACT.Copy, scale=rs[:, h : h + 1])
                nc.sync.dma_start(out=dst, in_=result[:])

        def norm_rope(acc, t, which, dst, keep_back):
            c_tab, s_tab = tables[which]
            squares = work.tile([P, BLOCK], F32)
            sums = work.tile([P, BLOCK_HEADS], F32)
            rs = late.tile([P, BLOCK_HEADS], F32)
            for h in range(BLOCK_HEADS):
                cols = slice(h * DH, (h + 1) * DH)
                nc.scalar.activation(out=squares[:, cols], in_=acc[:, cols], func=ACT.Square, accum_out=sums[:, h : h + 1])
            nc.scalar.activation(out=rs[:], in_=sums[:], func=ACT.Abs_reciprocal_sqrt, scale=1.0 / DH, bias=EPS)
            finish_scale(keep_back)
            t1 = work.tile([P, BLOCK], F32)
            t2 = work.tile([P, BLOCK], F32)
            heads = acc[:].rearrange("p (h d) -> p h d", h=BLOCK_HEADS)
            shape = [P, BLOCK_HEADS, DH]
            nc.vector.tensor_tensor(
                out=t1[:].rearrange("p (h d) -> p h d", h=BLOCK_HEADS),
                in0=heads, in1=c_tab[:, t, :].unsqueeze(1).to_broadcast(shape), op=ALU.mult,
            )
            finish_add()
            nc.vector.tensor_tensor(
                out=t2[:].rearrange("p (h d) -> p h d", h=BLOCK_HEADS),
                in0=heads, in1=s_tab[:, t, :].unsqueeze(1).to_broadcast(shape), op=ALU.mult,
            )
            to_add.append((t1, t2, rs, dst))

        def plain(acc, engine, width, dst, keep_back):
            copied = res.tile([P, BLOCK], F32)
            if engine == "scalar":
                nc.scalar.copy(out=copied[:, 0:width], in_=acc[:])
            else:
                nc.vector.tensor_copy(out=copied[:, 0:width], in_=acc[:])
            nc.sync.dma_start(out=dst, in_=copied[:, 0:width])
            finish_add()
            finish_scale(keep_back)

        def rows(t):
            return slice(P * t, P * (t + 1))

        for t in range(TOKEN_TILES):
            acc = psum.tile([P, BLOCK], F32, tag="acc")
            q1_accs.append(acc)
        for g in range(head):
            for t in range(TOKEN_TILES):
                mx_pass(q1_accs[t], g, t, q1_codes, q1_planes, 0, BLOCK)
        for t in range(TOKEN_TILES):
            for g in range(head, 4):
                mx_pass(q0_accs[t], g, t, q0_codes, q0_planes, 0, BLOCK)
        for accs, codes, planes, o0 in ((q0_accs, q0_codes, q0_planes, 0), (q1_accs, q1_codes, q1_planes, BLOCK)):
            for t in range(TOKEN_TILES):
                for g in range(4 if o0 == 0 else head, PASSES):
                    mx_pass(accs[t], g, t, codes, planes, 0, BLOCK)
                norm_rope(accs[t], t, "q", outs["q"][rows(t), o0 : o0 + BLOCK], 0)

        def product(codes, planes, t, c0, width):
            acc = psum.tile([P, width], F32, tag="acc")
            for g in range(PASSES):
                mx_pass(acc, g, t, codes, planes, c0, width)
            return acc

        for half in range(2):
            for t in range(TOKEN_TILES):
                acc = product(k_codes, k_planes, t, half * BLOCK, BLOCK)
                norm_rope(acc, t, "k", outs["k"][rows(t), half * BLOCK : (half + 1) * BLOCK], 1 + half)

        for t in range(TOKEN_TILES):
            acc = product(v_codes, v_planes, t, 0, BLOCK)
            plain(acc, "scalar", BLOCK, outs["v"][rows(t), 0:BLOCK], 3 if t == 0 else 0)
        for t, c0, width, engine in (
            (0, 512, 512, "scalar"),
            (1, 512, 512, "scalar"),
            (2, 512, 512, "vector"),
            (3, 512, 256, "scalar"),
            (3, 768, 128, "vector"),
            (3, 896, 128, "scalar"),
        ):
            acc = product(v_codes, v_planes, t, c0, width)
            plain(acc, engine, width, outs["v"][rows(t), c0 : c0 + width], 0)
